import numpy as np
import ml_dtypes


def mxq(x, axis, fmt="e4m3"):
    dtype, down = {"e4m3": (ml_dtypes.float8_e4m3fn, 7), "e5m2": (ml_dtypes.float8_e5m2, 14)}[fmt]
    v = np.moveaxis(np.asarray(x, np.float32).astype(ml_dtypes.bfloat16).astype(np.float64), axis, -1)
    blocks = v.reshape(v.shape[:-1] + (-1, 32))
    amax = np.abs(blocks).max(-1, keepdims=True)
    byte = np.maximum(np.where(amax > 0, np.frexp(amax)[1] - 1 + 127, 0) - down, 1)
    scale = np.exp2(byte - 127.0)
    codes = (blocks / scale).astype(np.float32).astype(dtype).astype(np.float64)
    return np.moveaxis((codes * scale).reshape(v.shape), -1, axis)


WIDE = False


def mx_kscale(k):
    if not WIDE:
        return np.ones(k)
    levels = np.array([10, -10, 5, -5, 0])
    a = np.random.permutation(np.resize(levels, k // 512 * 4)).reshape(k // 512, 4)
    idx = np.arange(k)
    return np.exp2(a[idx // 512, idx % 128 // 32])


BF16 = ml_dtypes.bfloat16


def bf(x):
    return np.asarray(x, np.float32).astype(BF16)


def f64(x):
    return np.asarray(x).astype(np.float64)


B, S, D, H, QL, KVL, RD, ND, VD = 2, 2048, 1024, 4, 512, 512, 64, 64, 128
QHD = ND + RD
ROPE_THETA, ROPE_RATIO = 10000.0, 1.0


def rope_tables(seq_len):
    half = RD // 2
    inv_freq = ROPE_RATIO / (ROPE_THETA ** (np.arange(half) * 2.0 / RD))
    freqs = np.arange(seq_len)[:, None] * inv_freq[None, :]
    return np.cos(freqs), np.sin(freqs)


def apply_rope(x, cos, sin):
    x_even = x[..., 0::2]
    x_odd = x[..., 1::2]
    r_even = x_even * cos - x_odd * sin
    r_odd = x_odd * cos + x_even * sin
    return np.stack([r_even, r_odd], axis=-1).reshape(x.shape)


def setup_inputs():
    s, t = mx_kscale(D), mx_kscale(QL)
    return {"hidden_states": bf(np.random.standard_normal((B, S, D)) * s),
            "Wqa": bf(np.random.standard_normal((D, QL)) / np.sqrt(D) / s[:, None] * t),
            "Wqb": bf(np.random.standard_normal((QL, H * QHD)) / np.sqrt(QL) / t[:, None])}


def reference(hidden_states, Wqa, Wqb):
    q_latent = mxq(f64(hidden_states), 2, "e4m3") @ mxq(f64(Wqa), 0, "e4m3")
    q = (mxq(q_latent, 2, "e4m3") @ mxq(f64(Wqb), 0, "e4m3")).reshape(B, S, H, QHD)
    q = q.transpose(0, 2, 1, 3)
    q_nope, q_pe = q[..., :ND], q[..., ND:]
    cos, sin = rope_tables(S)
    q_pe = apply_rope(q_pe, cos, sin)
    return np.concatenate([q_nope, q_pe], axis=-1)

@@ -1,0 +1,293 @@
+import math
+from contextlib import ExitStack
+
+import concourse.mybir as mybir
+from concourse.masks import make_identity
+
+F32 = mybir.dt.float32
+BF16 = mybir.dt.bfloat16
+I32 = mybir.dt.int32
+U32 = mybir.dt.uint32
+U8 = mybir.dt.uint8
+FP8X4 = mybir.dt.float8_e4m3fn_x4
+ALU = mybir.AluOpType
+FUNC = mybir.ActivationFunctionType
+
+P = 128
+PACK = 4
+BATCH, SEQ, D_MODEL, Q_LATENT = 2, 2048, 1024, 512
+HEADS, HEAD_DIM, NOPE_DIM = 4, 128, 64
+ROPE_DIM = HEAD_DIM - NOPE_DIM
+PAIRS = ROPE_DIM // 2
+ROPE_THETA = 10000.0
+
+K_PASS = P * PACK
+PASSES_A = D_MODEL // K_PASS
+WORDS = D_MODEL // 2
+LATENT_BLOCKS = Q_LATENT // P
+TILES_PER_BATCH = SEQ // P
+N_TILES = BATCH * TILES_PER_BATCH
+LOAD_TILES = 2
+STORE_TILES = 2
+RUN_TILES = 4
+LEAD_TILES = 3
+
+FLOPS = 2 * BATCH * SEQ * (D_MODEL * Q_LATENT + Q_LATENT * HEADS * HEAD_DIM)
+
+
+def tile_mlaattention_pa_t_kernel(tc, hidden_states, Wqa, Wqb, out):
+    nc = tc.nc
+    with ExitStack() as ctx:
+        ctx.enter_context(tc.manual_schedule())
+        const = ctx.enter_context(tc.tile_pool(name="const", bufs=1))
+        x_pool = ctx.enter_context(tc.tile_pool(name="x", bufs=N_TILES // LOAD_TILES))
+        xg_pool = ctx.enter_context(tc.tile_pool(name="xg", bufs=3))
+        xq_pool = ctx.enter_context(tc.tile_pool(name="xq", bufs=LEAD_TILES + 2))
+        lat_pool = ctx.enter_context(tc.tile_pool(name="lat", bufs=3))
+        rope_pool = ctx.enter_context(tc.tile_pool(name="rope", bufs=2))
+        out_pool = ctx.enter_context(tc.tile_pool(name="outp", bufs=4))
+        xt_psum = ctx.enter_context(tc.psum_pool(name="xt_psum", bufs=RUN_TILES))
+        lat_psum = ctx.enter_context(tc.psum_pool(name="lat_psum", bufs=2))
+        q_psum = ctx.enter_context(tc.psum_pool(name="q_psum", bufs=2))
+
+        wa_raw = const.tile([P, PASSES_A, PACK, Q_LATENT], BF16)
+        for c in range(PASSES_A):
+            nc.sync.dma_start(
+                out=wa_raw[:, c].rearrange("p (u e) n -> p u e n", u=2),
+                in_=Wqa[c * K_PASS : (c + 1) * K_PASS, :].rearrange("(u p e) n -> p u e n", u=2, e=2),
+            )
+        wb_raw = const.tile([P, PACK, Q_LATENT], BF16)
+        x_tiles = []
+        for g in range(N_TILES // LOAD_TILES):
+            b, t0 = divmod(g * LOAD_TILES, TILES_PER_BATCH)
+            x_sb = x_pool.tile([P, LOAD_TILES, D_MODEL], BF16)
+            nc.sync.dma_start(
+                out=x_sb[:],
+                in_=hidden_states[b].rearrange("(r t) k -> r t k", t=TILES_PER_BATCH)[:, t0 : t0 + LOAD_TILES, :],
+            )
+            x_tiles.append(x_sb)
+            if g == 1:
+                nc.sync.dma_start(out=wb_raw[:], in_=Wqb.rearrange("(p j) n -> p j n", j=PACK))
+
+        ident = const.tile([P, P], F32)
+        make_identity(nc, ident[:])
+        pos_i = const.tile([P, TILES_PER_BATCH], I32)
+        nc.gpsimd.iota(pos_i[:], pattern=[[1, TILES_PER_BATCH]], base=0, channel_multiplier=TILES_PER_BATCH)
+
+        warm = const.tile([P, 2], F32)
+        nc.vector.memset(warm[:], 0.0)
+        nc.scalar.activation(out=warm[:, 1:2], in_=warm[:, 0:1], func=FUNC.Sin)
+
+        pos_f = const.tile([P, TILES_PER_BATCH], F32)
+        nc.vector.tensor_copy(out=pos_f[:], in_=pos_i[:])
+        turns = const.tile([P, PAIRS, TILES_PER_BATCH], F32)
+        for i in range(PAIRS):
+            nc.vector.tensor_scalar_mul(
+                out=turns[:, i, :], in0=pos_f[:], scalar1=ROPE_THETA ** (-2.0 * i / ROPE_DIM) / (2.0 * math.pi)
+            )
+        turns_flat = turns[:].rearrange("p i t -> p (i t)")
+        whole_i = const.tile([P, PAIRS * TILES_PER_BATCH], I32)
+        nc.vector.tensor_copy(out=whole_i[:], in_=turns_flat)
+        whole_f = const.tile([P, PAIRS * TILES_PER_BATCH], F32)
+        nc.vector.tensor_copy(out=whole_f[:], in_=whole_i[:])
+        left = const.tile([P, PAIRS * TILES_PER_BATCH], F32)
+        nc.vector.tensor_tensor(out=left[:], in0=turns_flat, in1=whole_f[:], op=ALU.subtract)
+        minus = const.tile([P, PAIRS, TILES_PER_BATCH], F32)
+        minus_flat = minus[:].rearrange("p i t -> p (i t)")
+        nc.vector.scalar_tensor_tensor(
+            out=minus_flat, in0=left[:], scalar=0.5, in1=left[:], op0=ALU.is_gt, op1=ALU.subtract
+        )
+        sin_pm = const.tile([P, TILES_PER_BATCH, 2, PAIRS], F32)
+        minus_ti = minus[:].rearrange("p i t -> p t i")
+        nc.scalar.activation(out=sin_pm[:, :, 0, :], in_=minus_ti, func=FUNC.Sin, scale=2.0 * math.pi)
+        nc.scalar.activation(out=sin_pm[:, :, 1, :], in_=minus_ti, func=FUNC.Sin, scale=-2.0 * math.pi)
+        half_sin = const.tile([P, PAIRS * TILES_PER_BATCH], F32)
+        nc.scalar.activation(out=half_sin[:], in_=minus_flat, func=FUNC.Sin, scale=math.pi)
+        twice_sq = const.tile([P, PAIRS, TILES_PER_BATCH], F32)
+        nc.scalar.activation(
+            out=twice_sq[:].rearrange("p i t -> p (i t)"), in_=half_sin[:], func=FUNC.Square, scale=math.sqrt(2.0)
+        )
+        cos2 = const.tile([P, TILES_PER_BATCH, PAIRS, 2], F32)
+
+        wa_grouped = const.tile([P, PASSES_A, Q_LATENT, PACK], BF16, align_bytes=64)
+        wa_codes = const.tile([P, PASSES_A, Q_LATENT], U32, align_bytes=64)
+        wa_scales = const.tile([P, PASSES_A, Q_LATENT], U8, align_bytes=64)
+        for c in range(PASSES_A):
+            nc.vector.tensor_copy(
+                out=wa_grouped[:, c].rearrange("p (m q) t -> p m q t", m=LATENT_BLOCKS),
+                in_=wa_raw[:, c].rearrange("p t (q m) -> p m q t", m=LATENT_BLOCKS),
+            )
+        for c in range(PASSES_A):
+            nc.vector.quantize_mx(
+                out=wa_codes[:, c, :].bitcast(FP8X4),
+                scales=wa_scales[:, c, :],
+                in_=wa_grouped[:, c].rearrange("p n t -> p (n t)"),
+            )
+        wb_grouped = const.tile([P, Q_LATENT, PACK], BF16, align_bytes=64)
+        wb_codes = const.tile([P, Q_LATENT], U32, align_bytes=64)
+        wb_scales = const.tile([P, Q_LATENT], U8, align_bytes=64)
+
+        def prepare_wqb_and_cos():
+            nc.vector.tensor_copy(out=wb_grouped[:], in_=wb_raw[:].rearrange("p j n -> p n j"))
+            nc.vector.tensor_scalar(
+                out=cos2[:],
+                in0=twice_sq[:].rearrange("p i t -> p t i").unsqueeze(3).to_broadcast([P, TILES_PER_BATCH, PAIRS, 2]),
+                scalar1=-1.0,
+                scalar2=1.0,
+                op0=ALU.mult,
+                op1=ALU.add,
+            )
+            nc.vector.quantize_mx(
+                out=wb_codes[:].bitcast(FP8X4), scales=wb_scales[:], in_=wb_grouped[:].rearrange("p n j -> p (n j)")
+            )
+
+        xt_banks, xg_tiles, xq_tiles = {}, {}, {}
+        lat_banks, lat_tiles, latq_tiles = {}, {}, {}
+        q_banks, rope_tiles, out_tiles = {}, {}, {}
+
+        def transpose_x(n):
+            words = x_tiles[n // LOAD_TILES][:, n % LOAD_TILES, :].bitcast(F32)
+            xt = xt_psum.tile([P, WORDS // P, P], F32)
+            for w in range(WORDS // P):
+                nc.tensor.transpose(xt[:, w, :], words[:, w * P : (w + 1) * P], ident[:])
+            xt_banks[n] = xt
+
+        def copy_x(n):
+            xg = xg_pool.tile([P, PASSES_A, P, PACK], BF16, align_bytes=64)
+            nc.scalar.copy(
+                out=xg[:].rearrange("p c r t -> p c (r t)").bitcast(F32).rearrange("p c (r u) -> p c r u", u=2),
+                in_=xt_banks[n][:].rearrange("p (c u) r -> p c r u", u=2),
+            )
+            xg_tiles[n] = xg
+
+        def quantise_x(n):
+            x_codes = xq_pool.tile([P, PASSES_A, P], U32, align_bytes=64)
+            x_scales = xq_pool.tile([P, PASSES_A, P], U8, align_bytes=64)
+            nc.vector.quantize_mx(
+                out=x_codes[:].rearrange("p c r -> p (c r)").bitcast(FP8X4),
+                scales=x_scales[:].rearrange("p c r -> p (c r)"),
+                in_=xg_tiles[n][:].rearrange("p c r t -> p (c r t)"),
+            )
+            xq_tiles[n] = (x_codes, x_scales)
+
+        def first_matmul(n):
+            x_codes, x_scales = xq_tiles[n]
+            lat_ps = lat_psum.tile([P, LATENT_BLOCKS, P], F32)
+            for m in range(LATENT_BLOCKS):
+                for c in range(PASSES_A):
+                    nc.tensor.matmul_mx(
+                        out=lat_ps[:, m, :],
+                        lhsT=wa_codes[:, c, m * P : (m + 1) * P].bitcast(FP8X4),
+                        lhsT_scale=wa_scales[:, c, m * P : (m + 1) * P],
+                        rhs=x_codes[:, c, :].bitcast(FP8X4),
+                        rhs_scale=x_scales[:, c, :],
+                        start=(c == 0),
+                        stop=(c == PASSES_A - 1),
+                    )
+            lat_banks[n] = lat_ps
+
+        def copy_latent(n):
+            lat = lat_pool.tile([P, P, PACK], BF16, align_bytes=64)
+            nc.scalar.copy(out=lat[:], in_=lat_banks[n][:].rearrange("p m r -> p r m"))
+            lat_tiles[n] = lat
+
+        def quantise_latent(n):
+            lat_codes = lat_pool.tile([P, P], U32, align_bytes=64)
+            lat_scales = lat_pool.tile([P, P], U8, align_bytes=64)
+            nc.vector.quantize_mx(
+                out=lat_codes[:].bitcast(FP8X4), scales=lat_scales[:], in_=lat_tiles[n][:].rearrange("p r m -> p (r m)")
+            )
+            latq_tiles[n] = (lat_codes, lat_scales)
+
+        def second_matmul(n):
+            lat_codes, lat_scales = latq_tiles[n]
+            q_ps = q_psum.tile([P, HEADS, HEAD_DIM], F32)
+            nc.tensor.matmul_mx(
+                out=q_ps[:].rearrange("p h d -> p (h d)"),
+                lhsT=lat_codes[:].bitcast(FP8X4),
+                lhsT_scale=lat_scales[:],
+                rhs=wb_codes[:].bitcast(FP8X4),
+                rhs_scale=wb_scales[:],
+                start=True,
+                stop=True,
+            )
+            q_banks[n] = q_ps
+
+        def copy_nope(n):
+            if n % STORE_TILES == 0:
+                o_sb = out_pool.tile([P, HEADS, STORE_TILES, HEAD_DIM], F32)
+                out_tiles[n // STORE_TILES] = o_sb
+            o_sb = out_tiles[n // STORE_TILES]
+            nc.scalar.copy(out=o_sb[:, :, n % STORE_TILES, 0:NOPE_DIM], in_=q_banks[n][:, :, 0:NOPE_DIM])
+
+        def rope_products(n):
+            t = n % TILES_PER_BATCH
+            rotated = q_banks[n][:, :, NOPE_DIM:HEAD_DIM]
+            pairs = rotated.rearrange("p h (i e) -> p h i e", e=2)
+            by_cos = rope_pool.tile([P, HEADS, ROPE_DIM], F32)
+            by_sin = rope_pool.tile([P, 2, HEADS, PAIRS], F32)
+            nc.vector.tensor_tensor(
+                out=by_cos[:],
+                in0=rotated,
+                in1=cos2[:, t].rearrange("p i e -> p (i e)").unsqueeze(1).to_broadcast([P, HEADS, ROPE_DIM]),
+                op=ALU.mult,
+            )
+            for e in range(2):
+                nc.vector.tensor_tensor(
+                    out=by_sin[:, e],
+                    in0=pairs[:, :, :, 1 - e],
+                    in1=sin_pm[:, t, e, :].unsqueeze(1).to_broadcast([P, HEADS, PAIRS]),
+                    op=ALU.mult,
+                )
+            rope_tiles[n] = (by_cos, by_sin)
+
+        def rope_sum(n):
+            by_cos, by_sin = rope_tiles[n]
+            o_sb = out_tiles[n // STORE_TILES]
+            nc.vector.tensor_tensor(
+                out=o_sb[:, :, n % STORE_TILES, NOPE_DIM:HEAD_DIM].rearrange("p h (i e) -> p h i e", e=2),
+                in0=by_cos[:].rearrange("p h (i e) -> p h i e", e=2),
+                in1=by_sin[:].rearrange("p e h i -> p h i e"),
+                op=ALU.add,
+            )
+
+        def store(n_last):
+            b, t_last = divmod(n_last, TILES_PER_BATCH)
+            t0 = t_last - (STORE_TILES - 1)
+            nc.sync.dma_start(
+                out=out[b].rearrange("h (r t) d -> r h t d", t=TILES_PER_BATCH)[:, :, t0 : t0 + STORE_TILES, :],
+                in_=out_tiles[n_last // STORE_TILES][:],
+            )
+
+        def live(n):
+            return 0 <= n < N_TILES
+
+        def step(s):
+            ahead = s + LEAD_TILES
+            if live(ahead):
+                if ahead % RUN_TILES == 0:
+                    for n in range(ahead, ahead + RUN_TILES):
+                        transpose_x(n)
+                copy_x(ahead)
+            if live(s):
+                first_matmul(s)
+                copy_latent(s)
+            if live(s - 2):
+                second_matmul(s - 2)
+                copy_nope(s - 2)
+            if live(s - 1):
+                quantise_latent(s - 1)
+            if live(s - 3):
+                rope_products(s - 3)
+            if live(ahead - 1):
+                quantise_x(ahead - 1)
+            if live(s - 3):
+                rope_sum(s - 3)
+                if (s - 3) % STORE_TILES == STORE_TILES - 1:
+                    store(s - 3)
+
+        for s in range(-LEAD_TILES, 1):
+            step(s)
+        prepare_wqb_and_cos()
+        for s in range(1, N_TILES + 3):
+            step(s)

@@ -29,7 +29,7 @@ TILES_PER_BATCH = SEQ // P
 N_TILES = BATCH * TILES_PER_BATCH
 LOAD_TILES = 2
 STORE_TILES = 2
-RUN_TILES = 4
+RUN_TILES = 2
 LEAD_TILES = 3
 
 FLOPS = 2 * BATCH * SEQ * (D_MODEL * Q_LATENT + Q_LATENT * HEADS * HEAD_DIM)
@@ -41,14 +41,14 @@ def tile_mlaattention_pa_t_kernel(tc, hidden_states, Wqa, Wqb, out):
         ctx.enter_context(tc.manual_schedule())
         const = ctx.enter_context(tc.tile_pool(name="const", bufs=1))
         x_pool = ctx.enter_context(tc.tile_pool(name="x", bufs=N_TILES // LOAD_TILES))
-        xg_pool = ctx.enter_context(tc.tile_pool(name="xg", bufs=3))
+        xg_pool = ctx.enter_context(tc.tile_pool(name="xg", bufs=4))
         xq_pool = ctx.enter_context(tc.tile_pool(name="xq", bufs=LEAD_TILES + 2))
         lat_pool = ctx.enter_context(tc.tile_pool(name="lat", bufs=3))
         rope_pool = ctx.enter_context(tc.tile_pool(name="rope", bufs=2))
         out_pool = ctx.enter_context(tc.tile_pool(name="outp", bufs=4))
-        xt_psum = ctx.enter_context(tc.psum_pool(name="xt_psum", bufs=RUN_TILES))
+        xt_psum = ctx.enter_context(tc.psum_pool(name="xt_psum", bufs=3))
         lat_psum = ctx.enter_context(tc.psum_pool(name="lat_psum", bufs=2))
-        q_psum = ctx.enter_context(tc.psum_pool(name="q_psum", bufs=2))
+        q_psum = ctx.enter_context(tc.psum_pool(name="q_psum", bufs=3))
 
         wa_raw = const.tile([P, PASSES_A, PACK, Q_LATENT], BF16)
         for c in range(PASSES_A):

@@ -44,7 +44,7 @@ def tile_mlaattention_pa_t_kernel(tc, hidden_states, Wqa, Wqb, out):
         xg_pool = ctx.enter_context(tc.tile_pool(name="xg", bufs=4))
         xq_pool = ctx.enter_context(tc.tile_pool(name="xq", bufs=LEAD_TILES + 2))
         lat_pool = ctx.enter_context(tc.tile_pool(name="lat", bufs=3))
-        rope_pool = ctx.enter_context(tc.tile_pool(name="rope", bufs=2))
+        rope_pool = ctx.enter_context(tc.tile_pool(name="rope", bufs=4))
         out_pool = ctx.enter_context(tc.tile_pool(name="outp", bufs=4))
         xt_psum = ctx.enter_context(tc.psum_pool(name="xt_psum", bufs=3))
         lat_psum = ctx.enter_context(tc.psum_pool(name="lat_psum", bufs=2))
@@ -244,7 +244,7 @@ def tile_mlaattention_pa_t_kernel(tc, hidden_states, Wqa, Wqb, out):
         def rope_sum(n):
             by_cos, by_sin = rope_tiles[n]
             o_sb = out_tiles[n // STORE_TILES]
-            nc.vector.tensor_tensor(
+            nc.gpsimd.tensor_tensor(
                 out=o_sb[:, :, n % STORE_TILES, NOPE_DIM:HEAD_DIM].rearrange("p h (i e) -> p h i e", e=2),
                 in0=by_cos[:].rearrange("p h (i e) -> p h i e", e=2),
                 in1=by_sin[:].rearrange("p e h i -> p h i e"),

@@ -28,7 +28,6 @@ LATENT_BLOCKS = Q_LATENT // P
 TILES_PER_BATCH = SEQ // P
 N_TILES = BATCH * TILES_PER_BATCH
 LOAD_TILES = 2
-STORE_TILES = 2
 RUN_TILES = 2
 LEAD_TILES = 3
 
@@ -45,7 +44,7 @@ def tile_mlaattention_pa_t_kernel(tc, hidden_states, Wqa, Wqb, out):
         xq_pool = ctx.enter_context(tc.tile_pool(name="xq", bufs=LEAD_TILES + 2))
         lat_pool = ctx.enter_context(tc.tile_pool(name="lat", bufs=3))
         rope_pool = ctx.enter_context(tc.tile_pool(name="rope", bufs=4))
-        out_pool = ctx.enter_context(tc.tile_pool(name="outp", bufs=4))
+        out_pool = ctx.enter_context(tc.tile_pool(name="outp", bufs=6))
         xt_psum = ctx.enter_context(tc.psum_pool(name="xt_psum", bufs=3))
         lat_psum = ctx.enter_context(tc.psum_pool(name="lat_psum", bufs=2))
         q_psum = ctx.enter_context(tc.psum_pool(name="q_psum", bufs=3))
@@ -212,13 +211,14 @@ def tile_mlaattention_pa_t_kernel(tc, hidden_states, Wqa, Wqb, out):
                 stop=True,
             )
             q_banks[n] = q_ps
+            o_sb = out_pool.tile([P, HEADS, HEAD_DIM], F32)
+            out_tiles[n] = o_sb
 
         def copy_nope(n):
-            if n % STORE_TILES == 0:
-                o_sb = out_pool.tile([P, HEADS, STORE_TILES, HEAD_DIM], F32)
-                out_tiles[n // STORE_TILES] = o_sb
-            o_sb = out_tiles[n // STORE_TILES]
-            nc.scalar.copy(out=o_sb[:, :, n % STORE_TILES, 0:NOPE_DIM], in_=q_banks[n][:, :, 0:NOPE_DIM])
+            if n % 2 == 0:
+                nc.scalar.copy(out=out_tiles[n][:, :, 0:NOPE_DIM], in_=q_banks[n][:, :, 0:NOPE_DIM])
+            else:
+                nc.vector.tensor_copy(out=out_tiles[n][:, :, 0:NOPE_DIM], in_=q_banks[n][:, :, 0:NOPE_DIM])
 
         def rope_products(n):
             t = n % TILES_PER_BATCH
@@ -243,20 +243,17 @@ def tile_mlaattention_pa_t_kernel(tc, hidden_states, Wqa, Wqb, out):
 
         def rope_sum(n):
             by_cos, by_sin = rope_tiles[n]
-            o_sb = out_tiles[n // STORE_TILES]
             nc.gpsimd.tensor_tensor(
-                out=o_sb[:, :, n % STORE_TILES, NOPE_DIM:HEAD_DIM].rearrange("p h (i e) -> p h i e", e=2),
+                out=out_tiles[n][:, :, NOPE_DIM:HEAD_DIM].rearrange("p h (i e) -> p h i e", e=2),
                 in0=by_cos[:].rearrange("p h (i e) -> p h i e", e=2),
                 in1=by_sin[:].rearrange("p e h i -> p h i e"),
                 op=ALU.add,
             )
 
-        def store(n_last):
-            b, t_last = divmod(n_last, TILES_PER_BATCH)
-            t0 = t_last - (STORE_TILES - 1)
+        def store(n):
+            b, t = divmod(n, TILES_PER_BATCH)
             nc.sync.dma_start(
-                out=out[b].rearrange("h (r t) d -> r h t d", t=TILES_PER_BATCH)[:, :, t0 : t0 + STORE_TILES, :],
-                in_=out_tiles[n_last // STORE_TILES][:],
+                out=out[b].rearrange("h (r t) d -> r h t d", t=TILES_PER_BATCH)[:, :, t, :], in_=out_tiles[n][:]
             )
 
         def live(n):
@@ -274,17 +271,19 @@ def tile_mlaattention_pa_t_kernel(tc, hidden_states, Wqa, Wqb, out):
                 copy_latent(s)
             if live(s - 2):
                 second_matmul(s - 2)
-                copy_nope(s - 2)
+                if (s - 2) % 2 == 0:
+                    copy_nope(s - 2)
             if live(s - 1):
                 quantise_latent(s - 1)
             if live(s - 3):
                 rope_products(s - 3)
+                if (s - 3) % 2 == 1:
+                    copy_nope(s - 3)
             if live(ahead - 1):
                 quantise_x(ahead - 1)
             if live(s - 3):
                 rope_sum(s - 3)
-                if (s - 3) % STORE_TILES == STORE_TILES - 1:
-                    store(s - 3)
+                store(s - 3)
 
         for s in range(-LEAD_TILES, 1):
             step(s)

import math
from contextlib import ExitStack

import concourse.mybir as mybir
from concourse.masks import make_identity

F32 = mybir.dt.float32
BF16 = mybir.dt.bfloat16
I32 = mybir.dt.int32
U32 = mybir.dt.uint32
U8 = mybir.dt.uint8
FP8X4 = mybir.dt.float8_e4m3fn_x4
ALU = mybir.AluOpType
FUNC = mybir.ActivationFunctionType

P = 128
PACK = 4
BATCH, SEQ, D_MODEL, Q_LATENT = 2, 2048, 1024, 512
HEADS, HEAD_DIM, NOPE_DIM = 4, 128, 64
ROPE_DIM = HEAD_DIM - NOPE_DIM
PAIRS = ROPE_DIM // 2
ROPE_THETA = 10000.0

K_PASS = P * PACK
PASSES_A = D_MODEL // K_PASS
WORDS = D_MODEL // 2
LATENT_BLOCKS = Q_LATENT // P
TILES_PER_BATCH = SEQ // P
N_TILES = BATCH * TILES_PER_BATCH
LOAD_TILES = 2
RUN_TILES = 2
LEAD_TILES = 3

FLOPS = 2 * BATCH * SEQ * (D_MODEL * Q_LATENT + Q_LATENT * HEADS * HEAD_DIM)


def tile_mlaattention_pa_t_kernel(tc, hidden_states, Wqa, Wqb, out):
    nc = tc.nc
    with ExitStack() as ctx:
        ctx.enter_context(tc.manual_schedule())
        const = ctx.enter_context(tc.tile_pool(name="const", bufs=1))
        x_pool = ctx.enter_context(tc.tile_pool(name="x", bufs=N_TILES // LOAD_TILES))
        xg_pool = ctx.enter_context(tc.tile_pool(name="xg", bufs=4))
        xq_pool = ctx.enter_context(tc.tile_pool(name="xq", bufs=LEAD_TILES + 2))
        lat_pool = ctx.enter_context(tc.tile_pool(name="lat", bufs=3))
        rope_pool = ctx.enter_context(tc.tile_pool(name="rope", bufs=4))
        out_pool = ctx.enter_context(tc.tile_pool(name="outp", bufs=6))
        xt_psum = ctx.enter_context(tc.psum_pool(name="xt_psum", bufs=3))
        lat_psum = ctx.enter_context(tc.psum_pool(name="lat_psum", bufs=2))
        q_psum = ctx.enter_context(tc.psum_pool(name="q_psum", bufs=3))

        wa_raw = const.tile([P, PASSES_A, PACK, Q_LATENT], BF16)
        for c in range(PASSES_A):
            nc.sync.dma_start(
                out=wa_raw[:, c].rearrange("p (u e) n -> p u e n", u=2),
                in_=Wqa[c * K_PASS : (c + 1) * K_PASS, :].rearrange("(u p e) n -> p u e n", u=2, e=2),
            )
        wb_raw = const.tile([P, PACK, Q_LATENT], BF16)
        x_tiles = []
        for g in range(N_TILES // LOAD_TILES):
            b, t0 = divmod(g * LOAD_TILES, TILES_PER_BATCH)
            x_sb = x_pool.tile([P, LOAD_TILES, D_MODEL], BF16)
            nc.sync.dma_start(
                out=x_sb[:],
                in_=hidden_states[b].rearrange("(r t) k -> r t k", t=TILES_PER_BATCH)[:, t0 : t0 + LOAD_TILES, :],
            )
            x_tiles.append(x_sb)
            if g == 1:
                nc.sync.dma_start(out=wb_raw[:], in_=Wqb.rearrange("(p j) n -> p j n", j=PACK))

        ident = const.tile([P, P], F32)
        make_identity(nc, ident[:])
        pos_i = const.tile([P, TILES_PER_BATCH], I32)
        nc.gpsimd.iota(pos_i[:], pattern=[[1, TILES_PER_BATCH]], base=0, channel_multiplier=TILES_PER_BATCH)

        warm = const.tile([P, 2], F32)
        nc.vector.memset(warm[:], 0.0)
        nc.scalar.activation(out=warm[:, 1:2], in_=warm[:, 0:1], func=FUNC.Sin)

        pos_f = const.tile([P, TILES_PER_BATCH], F32)
        nc.vector.tensor_copy(out=pos_f[:], in_=pos_i[:])
        turns = const.tile([P, PAIRS, TILES_PER_BATCH], F32)
        for i in range(PAIRS):
            nc.vector.tensor_scalar_mul(
                out=turns[:, i, :], in0=pos_f[:], scalar1=ROPE_THETA ** (-2.0 * i / ROPE_DIM) / (2.0 * math.pi)
            )
        turns_flat = turns[:].rearrange("p i t -> p (i t)")
        whole_i = const.tile([P, PAIRS * TILES_PER_BATCH], I32)
        nc.vector.tensor_copy(out=whole_i[:], in_=turns_flat)
        whole_f = const.tile([P, PAIRS * TILES_PER_BATCH], F32)
        nc.vector.tensor_copy(out=whole_f[:], in_=whole_i[:])
        left = const.tile([P, PAIRS * TILES_PER_BATCH], F32)
        nc.vector.tensor_tensor(out=left[:], in0=turns_flat, in1=whole_f[:], op=ALU.subtract)
        minus = const.tile([P, PAIRS, TILES_PER_BATCH], F32)
        minus_flat = minus[:].rearrange("p i t -> p (i t)")
        nc.vector.scalar_tensor_tensor(
            out=minus_flat, in0=left[:], scalar=0.5, in1=left[:], op0=ALU.is_gt, op1=ALU.subtract
        )
        sin_pm = const.tile([P, TILES_PER_BATCH, 2, PAIRS], F32)
        minus_ti = minus[:].rearrange("p i t -> p t i")
        nc.scalar.activation(out=sin_pm[:, :, 0, :], in_=minus_ti, func=FUNC.Sin, scale=2.0 * math.pi)
        nc.scalar.activation(out=sin_pm[:, :, 1, :], in_=minus_ti, func=FUNC.Sin, scale=-2.0 * math.pi)
        half_sin = const.tile([P, PAIRS * TILES_PER_BATCH], F32)
        nc.scalar.activation(out=half_sin[:], in_=minus_flat, func=FUNC.Sin, scale=math.pi)
        twice_sq = const.tile([P, PAIRS, TILES_PER_BATCH], F32)
        nc.scalar.activation(
            out=twice_sq[:].rearrange("p i t -> p (i t)"), in_=half_sin[:], func=FUNC.Square, scale=math.sqrt(2.0)
        )
        cos2 = const.tile([P, TILES_PER_BATCH, PAIRS, 2], F32)

        wa_grouped = const.tile([P, PASSES_A, Q_LATENT, PACK], BF16, align_bytes=64)
        wa_codes = const.tile([P, PASSES_A, Q_LATENT], U32, align_bytes=64)
        wa_scales = const.tile([P, PASSES_A, Q_LATENT], U8, align_bytes=64)
        for c in range(PASSES_A):
            nc.vector.tensor_copy(
                out=wa_grouped[:, c].rearrange("p (m q) t -> p m q t", m=LATENT_BLOCKS),
                in_=wa_raw[:, c].rearrange("p t (q m) -> p m q t", m=LATENT_BLOCKS),
            )
        for c in range(PASSES_A):
            nc.vector.quantize_mx(
                out=wa_codes[:, c, :].bitcast(FP8X4),
                scales=wa_scales[:, c, :],
                in_=wa_grouped[:, c].rearrange("p n t -> p (n t)"),
            )
        wb_grouped = const.tile([P, Q_LATENT, PACK], BF16, align_bytes=64)
        wb_codes = const.tile([P, Q_LATENT], U32, align_bytes=64)
        wb_scales = const.tile([P, Q_LATENT], U8, align_bytes=64)

        def prepare_wqb_and_cos():
            nc.vector.tensor_copy(out=wb_grouped[:], in_=wb_raw[:].rearrange("p j n -> p n j"))
            nc.vector.tensor_scalar(
                out=cos2[:],
                in0=twice_sq[:].rearrange("p i t -> p t i").unsqueeze(3).to_broadcast([P, TILES_PER_BATCH, PAIRS, 2]),
                scalar1=-1.0,
                scalar2=1.0,
                op0=ALU.mult,
                op1=ALU.add,
            )
            nc.vector.quantize_mx(
                out=wb_codes[:].bitcast(FP8X4), scales=wb_scales[:], in_=wb_grouped[:].rearrange("p n j -> p (n j)")
            )

        xt_banks, xg_tiles, xq_tiles = {}, {}, {}
        lat_banks, lat_tiles, latq_tiles = {}, {}, {}
        q_banks, rope_tiles, out_tiles = {}, {}, {}

        def transpose_x(n):
            words = x_tiles[n // LOAD_TILES][:, n % LOAD_TILES, :].bitcast(F32)
            xt = xt_psum.tile([P, WORDS // P, P], F32)
            for w in range(WORDS // P):
                nc.tensor.transpose(xt[:, w, :], words[:, w * P : (w + 1) * P], ident[:])
            xt_banks[n] = xt

        def copy_x(n):
            xg = xg_pool.tile([P, PASSES_A, P, PACK], BF16, align_bytes=64)
            nc.scalar.copy(
                out=xg[:].rearrange("p c r t -> p c (r t)").bitcast(F32).rearrange("p c (r u) -> p c r u", u=2),
                in_=xt_banks[n][:].rearrange("p (c u) r -> p c r u", u=2),
            )
            xg_tiles[n] = xg

        def quantise_x(n):
            x_codes = xq_pool.tile([P, PASSES_A, P], U32, align_bytes=64)
            x_scales = xq_pool.tile([P, PASSES_A, P], U8, align_bytes=64)
            nc.vector.quantize_mx(
                out=x_codes[:].rearrange("p c r -> p (c r)").bitcast(FP8X4),
                scales=x_scales[:].rearrange("p c r -> p (c r)"),
                in_=xg_tiles[n][:].rearrange("p c r t -> p (c r t)"),
            )
            xq_tiles[n] = (x_codes, x_scales)

        def first_matmul(n):
            x_codes, x_scales = xq_tiles[n]
            lat_ps = lat_psum.tile([P, LATENT_BLOCKS, P], F32)
            for m in range(LATENT_BLOCKS):
                for c in range(PASSES_A):
                    nc.tensor.matmul_mx(
                        out=lat_ps[:, m, :],
                        lhsT=wa_codes[:, c, m * P : (m + 1) * P].bitcast(FP8X4),
                        lhsT_scale=wa_scales[:, c, m * P : (m + 1) * P],
                        rhs=x_codes[:, c, :].bitcast(FP8X4),
                        rhs_scale=x_scales[:, c, :],
                        start=(c == 0),
                        stop=(c == PASSES_A - 1),
                    )
            lat_banks[n] = lat_ps

        def copy_latent(n):
            lat = lat_pool.tile([P, P, PACK], BF16, align_bytes=64)
            nc.scalar.copy(out=lat[:], in_=lat_banks[n][:].rearrange("p m r -> p r m"))
            lat_tiles[n] = lat

        def quantise_latent(n):
            lat_codes = lat_pool.tile([P, P], U32, align_bytes=64)
            lat_scales = lat_pool.tile([P, P], U8, align_bytes=64)
            nc.vector.quantize_mx(
                out=lat_codes[:].bitcast(FP8X4), scales=lat_scales[:], in_=lat_tiles[n][:].rearrange("p r m -> p (r m)")
            )
            latq_tiles[n] = (lat_codes, lat_scales)

        def second_matmul(n):
            lat_codes, lat_scales = latq_tiles[n]
            q_ps = q_psum.tile([P, HEADS, HEAD_DIM], F32)
            nc.tensor.matmul_mx(
                out=q_ps[:].rearrange("p h d -> p (h d)"),
                lhsT=lat_codes[:].bitcast(FP8X4),
                lhsT_scale=lat_scales[:],
                rhs=wb_codes[:].bitcast(FP8X4),
                rhs_scale=wb_scales[:],
                start=True,
                stop=True,
            )
            q_banks[n] = q_ps
            o_sb = out_pool.tile([P, HEADS, HEAD_DIM], F32)
            out_tiles[n] = o_sb

        def copy_nope(n):
            if n % 2 == 0:
                nc.scalar.copy(out=out_tiles[n][:, :, 0:NOPE_DIM], in_=q_banks[n][:, :, 0:NOPE_DIM])
            else:
                nc.vector.tensor_copy(out=out_tiles[n][:, :, 0:NOPE_DIM], in_=q_banks[n][:, :, 0:NOPE_DIM])

        def rope_products(n):
            t = n % TILES_PER_BATCH
            rotated = q_banks[n][:, :, NOPE_DIM:HEAD_DIM]
            pairs = rotated.rearrange("p h (i e) -> p h i e", e=2)
            by_cos = rope_pool.tile([P, HEADS, ROPE_DIM], F32)
            by_sin = rope_pool.tile([P, 2, HEADS, PAIRS], F32)
            nc.vector.tensor_tensor(
                out=by_cos[:],
                in0=rotated,
                in1=cos2[:, t].rearrange("p i e -> p (i e)").unsqueeze(1).to_broadcast([P, HEADS, ROPE_DIM]),
                op=ALU.mult,
            )
            for e in range(2):
                nc.vector.tensor_tensor(
                    out=by_sin[:, e],
                    in0=pairs[:, :, :, 1 - e],
                    in1=sin_pm[:, t, e, :].unsqueeze(1).to_broadcast([P, HEADS, PAIRS]),
                    op=ALU.mult,
                )
            rope_tiles[n] = (by_cos, by_sin)

        def rope_sum(n):
            by_cos, by_sin = rope_tiles[n]
            nc.gpsimd.tensor_tensor(
                out=out_tiles[n][:, :, NOPE_DIM:HEAD_DIM].rearrange("p h (i e) -> p h i e", e=2),
                in0=by_cos[:].rearrange("p h (i e) -> p h i e", e=2),
                in1=by_sin[:].rearrange("p e h i -> p h i e"),
                op=ALU.add,
            )

        def store(n):
            b, t = divmod(n, TILES_PER_BATCH)
            nc.sync.dma_start(
                out=out[b].rearrange("h (r t) d -> r h t d", t=TILES_PER_BATCH)[:, :, t, :], in_=out_tiles[n][:]
            )

        def live(n):
            return 0 <= n < N_TILES

        def step(s):
            ahead = s + LEAD_TILES
            if live(ahead):
                if ahead % RUN_TILES == 0:
                    for n in range(ahead, ahead + RUN_TILES):
                        transpose_x(n)
                copy_x(ahead)
            if live(s):
                first_matmul(s)
                copy_latent(s)
            if live(s - 2):
                second_matmul(s - 2)
                if (s - 2) % 2 == 0:
                    copy_nope(s - 2)
            if live(s - 1):
                quantise_latent(s - 1)
            if live(s - 3):
                rope_products(s - 3)
                if (s - 3) % 2 == 1:
                    copy_nope(s - 3)
            if live(ahead - 1):
                quantise_x(ahead - 1)
            if live(s - 3):
                rope_sum(s - 3)
                store(s - 3)

        for s in range(-LEAD_TILES, 1):
            step(s)
        prepare_wqb_and_cos()
        for s in range(1, N_TILES + 3):
            step(s)
